import numpy as np
import ml_dtypes


def mxq(x, axis, fmt="e4m3"):
    dtype, down = {"e4m3": (ml_dtypes.float8_e4m3fn, 7), "e5m2": (ml_dtypes.float8_e5m2, 14)}[fmt]
    v = np.moveaxis(np.asarray(x, np.float32).astype(ml_dtypes.bfloat16).astype(np.float64), axis, -1)
    blocks = v.reshape(v.shape[:-1] + (-1, 32))
    amax = np.abs(blocks).max(-1, keepdims=True)
    byte = np.maximum(np.where(amax > 0, np.frexp(amax)[1] - 1 + 127, 0) - down, 1)
    scale = np.exp2(byte - 127.0)
    codes = (blocks / scale).astype(np.float32).astype(dtype).astype(np.float64)
    return np.moveaxis((codes * scale).reshape(v.shape), -1, axis)


WIDE = False


def mx_kscale(k):
    if not WIDE:
        return np.ones(k)
    levels = np.array([10, -10, 5, -5, 0])
    if k % 512:
        return np.exp2(np.random.permutation(np.resize(levels, k // 32))).repeat(32)
    a = np.empty((k // 512, 16))
    for p in range(k // 512):
        a[p, :8] = np.random.permutation(np.resize(levels, 8))
        for g in range(8):
            far = levels[np.abs(levels - a[p, g]) >= 10]
            a[p, g + 8] = far[np.random.randint(len(far))]
    return np.exp2(a.ravel()).repeat(32)


BF16 = ml_dtypes.bfloat16


def bf(x):
    return np.asarray(x, np.float32).astype(BF16)


def f64(x):
    return np.asarray(x).astype(np.float64)


E2M1 = np.array([0.0, 0.5, 1.0, 1.5, 2.0, 3.0, 4.0, 6.0, -0.0, -0.5, -1.0, -1.5, -2.0, -3.0, -4.0, -6.0])


def pack_weight(w, fmt):
    k, n = w.shape
    w = f64(bf(w)).reshape(k // 32, 32, n)
    amax = np.abs(w).max(1)
    if fmt == "e4m3":
        byte = np.frexp(amax)[1] - 1 + 127 - 7
    else:
        mant, ex = np.frexp(amax / 6.0)
        byte = np.where(mant > 0.5, ex, ex - 1) + 127
    byte = np.clip(np.where(amax > 0, byte, 1), 1, 254)
    scaled = (w * np.exp2(127.0 - byte)[:, None, :]).reshape(k, n).astype(np.float32)
    by_word = np.ascontiguousarray(scaled.reshape(k // 512, 128, 4, n).transpose(0, 1, 3, 2))
    if fmt == "e4m3":
        words = by_word.astype(ml_dtypes.float8_e4m3fn).view(np.uint8)
    else:
        c = by_word.astype(ml_dtypes.float4_e2m1fn).view(np.uint8) & 0xF
        words = c[..., 0::2] | (c[..., 1::2] << 4)
    return np.ascontiguousarray(words), np.ascontiguousarray(byte.astype(np.uint8).reshape(k // 512, 16, n))


def unpack_weight(words, scales, fmt):
    g, p, n, _ = words.shape
    if fmt == "e4m3":
        vals = np.ascontiguousarray(words).view(ml_dtypes.float8_e4m3fn).astype(np.float64)
    else:
        nib = np.empty((g, p, n, 4), np.uint8)
        nib[..., 0::2] = words & 0xF
        nib[..., 1::2] = words >> 4
        vals = E2M1[nib]
    vals = vals * np.repeat(np.exp2(scales.astype(np.float64) - 127.0), 8, axis=1)[..., None]
    return vals.transpose(0, 1, 3, 2).reshape(g * 512, n)
def pack4(w):
    words, scales = pack_weight(w, "e2m1")
    return words.reshape(words.shape[0], 128, -1), scales


def unpack4(words, scales):
    return unpack_weight(words.reshape(words.shape[0], 128, -1, 2), scales, "e2m1")


B, S, NS, DS, H = 4, 1024, 4, 128, 512
D = NS * DS


def draw0():
    t, u = mx_kscale(H), mx_kscale(D)
    hid = bf(0.6 * np.random.standard_normal((B, S, NS, H)) * t)
    Wd = bf(1.5 * np.random.standard_normal((NS, H, DS)) / np.sqrt(H) / t[None, :, None] * u.reshape(NS, 1, DS))
    words, scales = pack4(np.random.standard_normal((D, D)) / np.sqrt(D) / u[:, None])
    return {"hid": hid,
            "Wd": Wd,
            "Wo_words": words,
            "Wo_scales": scales,
            "x": bf(np.random.standard_normal((B, S, D)))}


def core(hid, Wd, Wo_words, Wo_scales, x):
    hq = mxq(f64(hid).transpose(0, 2, 1, 3), 3, "e4m3")
    down = hq @ mxq(f64(Wd), 1, "e4m3")
    joined = down.transpose(0, 2, 1, 3).reshape(B, S, D)
    return (mxq(joined, 2, "e4m3") @ unpack4(Wo_words, Wo_scales)) + f64(x)


def e4m3fn_bytes(y):
    return np.clip(np.asarray(y, np.float64), -448.0, 448.0).astype(np.float32).astype(ml_dtypes.float8_e4m3fn).view(np.uint8)


def e4m3fn_values(b):
    return np.asarray(b, np.uint8).view(ml_dtypes.float8_e4m3fn).astype(np.float64)


def setup_inputs():
    d = draw0()
    x0 = np.asarray(d['hid']).astype(np.float64)
    s = (np.max(np.abs(x0), axis=(0, 1, 2), keepdims=True) / 448.0).astype(np.float32)
    out = {}
    for k, v in d.items():
        if k == 'hid':
            out['hid_bytes'] = e4m3fn_bytes(x0 / s.astype(np.float64))
            out['hid_scale'] = s
        else:
            out[k] = v
    return out


def reference(hid_bytes, hid_scale, Wd, Wo_words, Wo_scales, x):
    return core(e4m3fn_values(hid_bytes) * hid_scale.astype(np.float64), Wd, Wo_words, Wo_scales, x)

@@ -1,0 +1,211 @@
+import concourse.mybir as mybir
+from concourse.masks import make_identity
+from contextlib import ExitStack
+
+F32 = mybir.dt.float32
+BF16 = mybir.dt.bfloat16
+U32 = mybir.dt.uint32
+I32 = mybir.dt.int32
+U8 = mybir.dt.uint8
+F8 = mybir.dt.float8_e4m3fn
+F8X4 = mybir.dt.float8_e4m3fn_x4
+F4X4 = mybir.dt.float4_e2m1fn_x4
+MULT = mybir.AluOpType.mult
+ADD = mybir.AluOpType.add
+
+P = 128
+TOKENS = 4096
+NS = 4
+H = 512
+DS = 128
+D = NS * DS
+TILES = TOKENS // P
+PAIRS = TILES // 2
+FLOPS = 2 * TOKENS * NS * H * DS + 2 * TOKENS * D * D
+
+
+def tile_mopn_layer_pb_t_w4_kernel(tc, hid_bytes, hid_scale, Wd, Wo_words, Wo_scales, x, out):
+    nc = tc.nc
+    hid = hid_bytes.rearrange("b s n k -> (b s) (n k)").rearrange("(j p i) c -> j p (i c)", p=P, i=2)
+    xin = x.rearrange("b s d -> (b s) d").rearrange("(j p i) c -> j p (i c)", p=P, i=2)
+    oview = out.rearrange("b s d -> (b s) d").rearrange("(j p i) c -> j p (i c)", p=P, i=2)
+    srow = hid_scale.rearrange("a b c k -> (a b c k)")
+
+    with ExitStack() as ctx:
+        keep = ctx.enter_context(tc.tile_pool(name="keep", bufs=1))
+        loads = ctx.enter_context(tc.tile_pool(name="loads", bufs=8))
+        sb = ctx.enter_context(tc.tile_pool(name="sb", bufs=3))
+        pst = ctx.enter_context(tc.psum_pool(name="pst", bufs=2))
+
+        ctx.enter_context(tc.manual_schedule())
+
+        scale = keep.tile([P, NS * H], F32, align_bytes=64)
+        ident = keep.tile([P, P], F32, align_bytes=64)
+        w_raw = keep.tile([P, NS, 4, DS], BF16, align_bytes=64)
+        w_grp = keep.tile([P, NS, 4, 32, 4], BF16, align_bytes=64)
+        w_codes = keep.tile([P, NS, 4, 32], U32, align_bytes=64)
+        w_scales = keep.tile([P, NS, 4, 32], U8, align_bytes=64)
+        wz_codes = keep.tile([P, 4, NS, P], U32, align_bytes=64)
+        wz_scales = keep.tile([P, 4, NS, P], U8, align_bytes=64)
+        wo_words = keep.tile([P, 2 * D], U8, align_bytes=64)
+        wo_scales = keep.tile([P, D], U8, align_bytes=64)
+
+        hbs = {}
+        xts = {}
+
+        def load_hid(j, halves=1):
+            hb = loads.tile([P, 4096], U8, align_bytes=64)
+            w = 4096 // halves
+            for h in range(halves):
+                nc.sync.dma_start(out=hb[:, h * w : (h + 1) * w], in_=hid[j][:, h * w : (h + 1) * w])
+            hbs[j] = hb
+
+        def load_x(j):
+            xt = loads.tile([P, 2 * D], BF16, align_bytes=64)
+            nc.sync.dma_start(out=xt[:], in_=xin[j])
+            xts[j] = xt
+
+        nc.sync.dma_start(out=scale[:, 0:H], in_=srow.partition_broadcast(P))
+        load_hid(0, 2)
+        nc.sync.dma_start(out=w_raw[:].rearrange("p n j d -> p n (j d)"), in_=Wd.rearrange("n (p j) d -> p n (j d)", j=4))
+        nc.gpsimd.memset(w_scales[:].rearrange("p n t m -> p (n t m)").bitcast(I32), 0)
+        nc.gpsimd.memset(wo_scales[:].bitcast(I32), 0)
+        make_identity(nc, ident[:])
+        nc.gpsimd.memset(wz_scales[:].rearrange("p t n m -> p (t n m)").bitcast(I32), 0)
+        nc.gpsimd.memset(wz_codes[:].rearrange("p t n m -> p (t n m)").bitcast(I32), 0)
+        load_hid(1)
+        nc.sync.dma_start(out=wo_words[:], in_=Wo_words[0])
+        wos = Wo_scales[0].bitcast(I32)
+        for q in range(4):
+            nc.sync.dma_start(out=wo_scales[32 * q : 32 * q + 4, :].bitcast(I32), in_=wos[4 * q : 4 * q + 4, :])
+        load_x(0)
+        for j in range(2, 5):
+            load_hid(j)
+            load_x(j - 1)
+
+        for n in range(1, NS):
+            nc.scalar.copy(out=scale[:, n * H : (n + 1) * H], in_=scale[:, 0:H])
+        for n in range(NS):
+            nc.scalar.copy(out=w_grp[:, n], in_=w_raw[:, n].rearrange("p j (m t) -> p t m j", t=4))
+
+        def prepare_w():
+            nc.vector.quantize_mx(
+                out=w_codes[:].rearrange("p n t m -> p (n t m)").bitcast(F8X4),
+                scales=w_scales[:].rearrange("p n t m -> p (n t m)"),
+                in_=w_grp[:].rearrange("p n t m j -> p (n t m j)"),
+            )
+            for n in range(NS):
+                nc.vector.tensor_copy(out=wz_codes[:, :, n, 32 * n : 32 * n + 32].bitcast(I32), in_=w_codes[:, n].bitcast(I32))
+                nc.vector.tensor_copy(out=wz_scales[:, :, n, 32 * n : 32 * n + 32], in_=w_scales[:, n])
+
+        xs_t, xt_t, g_t, c_t, s_t, jp_t, jg_t, jc_t, js_t, po_t, o_t = ({} for z in range(11))
+
+        def widen(i):
+            xs = sb.tile([P, NS * H], BF16, align_bytes=64)
+            base = (i % 2) * NS * H
+            hb = hbs[i // 2]
+            w = 512 if i == 0 else 2048
+            for c in range(0, 2048, w):
+                nc.vector.tensor_tensor(
+                    out=xs[:, c : c + w],
+                    in0=hb[:, base + c : base + c + w].bitcast(F8),
+                    in1=scale[:, 0:w],
+                    op=MULT,
+                )
+            xs_t[i] = xs
+
+        def turn(i):
+            words = xs_t[i][:].bitcast(F32)
+            banks = []
+            for h in range(2):
+                xt = pst.tile([P, 2, 2, P], F32, name="xt%d" % h)
+                for a in range(2):
+                    n = 2 * h + a
+                    for u in range(2):
+                        nc.tensor.transpose(xt[:, a, u, :], words[:, 256 * n + u : 256 * (n + 1) : 2], ident[:])
+                banks.append(xt)
+            xt_t[i] = banks
+
+        def empty(i):
+            g = sb.tile([P, 2048], BF16, align_bytes=64)
+            for h in range(2):
+                nc.scalar.copy(
+                    out=g[:, 1024 * h : 1024 * (h + 1)].bitcast(F32).rearrange("p (a r u) -> p a r u", a=2, u=2),
+                    in_=xt_t[i][h][:].rearrange("p a u r -> p a r u"),
+                )
+            g_t[i] = g
+
+        def quant(i):
+            c = sb.tile([P, 512], U32, name="codes", align_bytes=64)
+            s = sb.tile([P, 512], U8, name="scales", align_bytes=64)
+            nc.vector.quantize_mx(out=c[:].bitcast(F8X4), scales=s[:], in_=g_t[i][:])
+            c_t[i], s_t[i] = c, s
+
+        def mm1(i):
+            jp = pst.tile([P, 4, P], F32, name="jp")
+            for t in range(4):
+                for n in range(NS):
+                    nc.tensor.matmul_mx(
+                        out=jp[:, t, :],
+                        lhsT=wz_codes[:, t, n, :].bitcast(F8X4),
+                        lhsT_scale=wz_scales[:, t, n, :],
+                        rhs=c_t[i][:, P * n : P * (n + 1)].bitcast(F8X4),
+                        rhs_scale=s_t[i][:, P * n : P * (n + 1)],
+                        start=(n == 0),
+                        stop=(n == NS - 1),
+                    )
+            jp_t[i] = jp
+
+        def empty_j(i):
+            jg = sb.tile([P, P, 4], BF16, name="jg", align_bytes=64)
+            nc.scalar.copy(out=jg[:], in_=jp_t[i][:].rearrange("p t r -> p r t"))
+            jg_t[i] = jg
+
+        def quant_j(i):
+            c = sb.tile([P, P], U32, name="jcodes", align_bytes=64)
+            s = sb.tile([P, P], U8, name="jscales", align_bytes=64)
+            nc.vector.quantize_mx(out=c[:].bitcast(F8X4), scales=s[:], in_=jg_t[i][:].rearrange("p r t -> p (r t)"))
+            jc_t[i], js_t[i] = c, s
+
+        def mm2(i):
+            po = pst.tile([P, D], F32, name="po")
+            nc.tensor.matmul_mx(
+                out=po[:],
+                lhsT=jc_t[i][:].bitcast(F8X4),
+                lhsT_scale=js_t[i][:],
+                rhs=wo_words[:].bitcast(F4X4),
+                rhs_scale=wo_scales[:],
+                start=True,
+                stop=True,
+            )
+            po_t[i] = po
+
+        def add(i):
+            if i % 2 == 0:
+                o_t[i // 2] = sb.tile([P, 2 * D], F32, name="o", align_bytes=64)
+            o = o_t[i // 2]
+            cols = slice((i % 2) * D, (i % 2 + 1) * D)
+            nc.vector.tensor_tensor(out=o[:, cols], in0=po_t[i][:], in1=xts[i // 2][:, cols], op=ADD)
+            if i % 2 == 1:
+                nc.sync.dma_start(out=oview[i // 2], in_=o[:])
+
+        for i in range(TILES + 3):
+            if i % 2 == 0 and i // 2 + 5 < PAIRS:
+                load_hid(i // 2 + 5)
+            if i % 2 == 0 and i // 2 + 4 < PAIRS:
+                load_x(i // 2 + 4)
+            if i < TILES:
+                widen(i)
+                turn(i)
+                empty(i)
+            if i == 1:
+                prepare_w()
+            if 0 <= i - 1 < TILES:
+                quant(i - 1)
+                mm1(i - 1)
+                empty_j(i - 1)
+            if 0 <= i - 2 < TILES:
+                quant_j(i - 2)
+                mm2(i - 2)
+            if 0 <= i - 3 < TILES:
+                add(i - 3)

@@ -34,19 +34,20 @@ def tile_mopn_layer_pb_t_w4_kernel(tc, hid_bytes, hid_scale, Wd, Wo_words, Wo_sc
     with ExitStack() as ctx:
         keep = ctx.enter_context(tc.tile_pool(name="keep", bufs=1))
         loads = ctx.enter_context(tc.tile_pool(name="loads", bufs=8))
-        sb = ctx.enter_context(tc.tile_pool(name="sb", bufs=3))
+        sb = ctx.enter_context(tc.tile_pool(name="sb", bufs=4))
         pst = ctx.enter_context(tc.psum_pool(name="pst", bufs=2))
 
         ctx.enter_context(tc.manual_schedule())
 
         scale = keep.tile([P, NS * H], F32, align_bytes=64)
+        scale_p = keep.tile([P, 4], F32, align_bytes=64)
         ident = keep.tile([P, P], F32, align_bytes=64)
+        ident_b = keep.tile([P, P], BF16, align_bytes=64)
         w_raw = keep.tile([P, NS, 4, DS], BF16, align_bytes=64)
-        w_grp = keep.tile([P, NS, 4, 32, 4], BF16, align_bytes=64)
-        w_codes = keep.tile([P, NS, 4, 32], U32, align_bytes=64)
-        w_scales = keep.tile([P, NS, 4, 32], U8, align_bytes=64)
+        w_grp = keep.tile([P, 4, NS, 32, 4], BF16, align_bytes=64)
+        w_codes = keep.tile([P, 4, NS, 32], U32, align_bytes=64)
+        w_scales = keep.tile([P, 4 * P], U8, align_bytes=64)
         wz_codes = keep.tile([P, 4, NS, P], U32, align_bytes=64)
-        wz_scales = keep.tile([P, 4, NS, P], U8, align_bytes=64)
         wo_words = keep.tile([P, 2 * D], U8, align_bytes=64)
         wo_scales = keep.tile([P, D], U8, align_bytes=64)
 
@@ -68,12 +69,12 @@ def tile_mopn_layer_pb_t_w4_kernel(tc, hid_bytes, hid_scale, Wd, Wo_words, Wo_sc
         nc.sync.dma_start(out=scale[:, 0:H], in_=srow.partition_broadcast(P))
         load_hid(0, 2)
         nc.sync.dma_start(out=w_raw[:].rearrange("p n j d -> p n (j d)"), in_=Wd.rearrange("n (p j) d -> p n (j d)", j=4))
-        nc.gpsimd.memset(w_scales[:].rearrange("p n t m -> p (n t m)").bitcast(I32), 0)
         nc.gpsimd.memset(wo_scales[:].bitcast(I32), 0)
         make_identity(nc, ident[:])
-        nc.gpsimd.memset(wz_scales[:].rearrange("p t n m -> p (t n m)").bitcast(I32), 0)
+        make_identity(nc, ident_b[:])
         nc.gpsimd.memset(wz_codes[:].rearrange("p t n m -> p (t n m)").bitcast(I32), 0)
         load_hid(1)
+        nc.sync.dma_start(out=scale_p[:], in_=srow.rearrange("(p t) -> p t", t=4))
         nc.sync.dma_start(out=wo_words[:], in_=Wo_words[0])
         wos = Wo_scales[0].bitcast(I32)
         for q in range(4):
@@ -86,26 +87,38 @@ def tile_mopn_layer_pb_t_w4_kernel(tc, hid_bytes, hid_scale, Wd, Wo_words, Wo_sc
         for n in range(1, NS):
             nc.scalar.copy(out=scale[:, n * H : (n + 1) * H], in_=scale[:, 0:H])
         for n in range(NS):
-            nc.scalar.copy(out=w_grp[:, n], in_=w_raw[:, n].rearrange("p j (m t) -> p t m j", t=4))
+            nc.scalar.copy(out=w_grp[:, :, n], in_=w_raw[:, n].rearrange("p j (m t) -> p t m j", t=4))
 
         def prepare_w():
             nc.vector.quantize_mx(
-                out=w_codes[:].rearrange("p n t m -> p (n t m)").bitcast(F8X4),
-                scales=w_scales[:].rearrange("p n t m -> p (n t m)"),
-                in_=w_grp[:].rearrange("p n t m j -> p (n t m j)"),
+                out=w_codes[:].rearrange("p t n m -> p (t n m)").bitcast(F8X4),
+                scales=w_scales[:],
+                in_=w_grp[:].rearrange("p t n m j -> p (t n m j)"),
             )
             for n in range(NS):
-                nc.vector.tensor_copy(out=wz_codes[:, :, n, 32 * n : 32 * n + 32].bitcast(I32), in_=w_codes[:, n].bitcast(I32))
-                nc.vector.tensor_copy(out=wz_scales[:, :, n, 32 * n : 32 * n + 32], in_=w_scales[:, n])
+                nc.vector.tensor_copy(out=wz_codes[:, :, n, 32 * n : 32 * n + 32].bitcast(I32), in_=w_codes[:, :, n].bitcast(I32))
 
         xs_t, xt_t, g_t, c_t, s_t, jp_t, jg_t, jc_t, js_t, po_t, o_t = ({} for z in range(11))
+
+        ws_t = {}
+
+        def on_scalar(i):
+            return 2 <= i < TILES - 2 and i % 3 != 1
+
+        def widen_s(i):
+            if not on_scalar(i):
+                return
+            ws = sb.tile([P, H], BF16, align_bytes=64)
+            base = (i % 2) * NS * H + 3 * H
+            nc.scalar.copy(out=ws[:], in_=hbs[i // 2][:, base : base + H].bitcast(F8))
+            ws_t[i] = ws
 
         def widen(i):
             xs = sb.tile([P, NS * H], BF16, align_bytes=64)
             base = (i % 2) * NS * H
             hb = hbs[i // 2]
-            w = 512 if i == 0 else 2048
-            for c in range(0, 2048, w):
+            w = 512 if i == 0 else 1024 if i == TILES - 1 else 1536 if on_scalar(i) else 2048
+            for c in range(0, 3 * H if on_scalar(i) else 4 * H, w):
                 nc.vector.tensor_tensor(
                     out=xs[:, c : c + w],
                     in0=hb[:, base + c : base + c + w].bitcast(F8),
@@ -121,6 +134,11 @@ def tile_mopn_layer_pb_t_w4_kernel(tc, hid_bytes, hid_scale, Wd, Wo_words, Wo_sc
                 xt = pst.tile([P, 2, 2, P], F32, name="xt%d" % h)
                 for a in range(2):
                     n = 2 * h + a
+                    if n == 3 and on_scalar(i):
+                        planes = xt[:, a].rearrange("p u r -> p (u r)").bitcast(BF16)
+                        for t in range(4):
+                            nc.tensor.transpose(planes[:, P * t : P * (t + 1)], ws_t[i][:, t::4], ident_b[:])
+                        continue
                     for u in range(2):
                         nc.tensor.transpose(xt[:, a, u, :], words[:, 256 * n + u : 256 * (n + 1) : 2], ident[:])
                 banks.append(xt)
@@ -129,6 +147,21 @@ def tile_mopn_layer_pb_t_w4_kernel(tc, hid_bytes, hid_scale, Wd, Wo_words, Wo_sc
         def empty(i):
             g = sb.tile([P, 2048], BF16, align_bytes=64)
             for h in range(2):
+                if h == 1 and on_scalar(i):
+                    nc.scalar.copy(
+                        out=g[:, 1024:1536].bitcast(F32).rearrange("p (r u) -> p r u", u=2),
+                        in_=xt_t[i][1][:, 0].rearrange("p u r -> p r u"),
+                    )
+                    planes = xt_t[i][1][:, 1].rearrange("p u r -> p (u r)").bitcast(BF16)
+                    dst = g[:, 1536:2048].rearrange("p (r t) -> p r t", t=4)
+                    for t in range(4):
+                        nc.scalar.activation(
+                            out=dst[:, :, t],
+                            in_=planes[:, P * t : P * (t + 1)],
+                            func=mybir.ActivationFunctionType.Copy,
+                            scale=scale_p[:, t : t + 1],
+                        )
+                    continue
                 nc.scalar.copy(
                     out=g[:, 1024 * h : 1024 * (h + 1)].bitcast(F32).rearrange("p (a r u) -> p a r u", a=2, u=2),
                     in_=xt_t[i][h][:].rearrange("p a u r -> p a r u"),
@@ -148,7 +181,7 @@ def tile_mopn_layer_pb_t_w4_kernel(tc, hid_bytes, hid_scale, Wd, Wo_words, Wo_sc
                     nc.tensor.matmul_mx(
                         out=jp[:, t, :],
                         lhsT=wz_codes[:, t, n, :].bitcast(F8X4),
-                        lhsT_scale=wz_scales[:, t, n, :],
+                        lhsT_scale=w_scales[:, P * t : P * (t + 1)],
                         rhs=c_t[i][:, P * n : P * (n + 1)].bitcast(F8X4),
                         rhs_scale=s_t[i][:, P * n : P * (n + 1)],
                         start=(n == 0),
@@ -186,26 +219,19 @@ def tile_mopn_layer_pb_t_w4_kernel(tc, hid_bytes, hid_scale, Wd, Wo_words, Wo_sc
             o = o_t[i // 2]
             cols = slice((i % 2) * D, (i % 2 + 1) * D)
             nc.vector.tensor_tensor(out=o[:, cols], in0=po_t[i][:], in1=xts[i // 2][:, cols], op=ADD)
-            if i % 2 == 1:
+            if i >= TILES - 2:
+                nc.sync.dma_start(out=oview[i // 2][:, cols], in_=o[:, cols])
+            elif i % 2 == 1:
                 nc.sync.dma_start(out=oview[i // 2], in_=o[:])
 
-        for i in range(TILES + 3):
-            if i % 2 == 0 and i // 2 + 5 < PAIRS:
+        STAGES = [(empty_j, 3), (widen_s, -1), (widen, 0), (add, 6), (quant, 2), (quant_j, 4), (turn, 0), (empty, 0), (mm1, 2), (mm2, 4)]
+        for i in range(-1, TILES + 6):
+            if i % 2 == 0 and i // 2 + 5 < PAIRS and i >= 0:
                 load_hid(i // 2 + 5)
-            if i % 2 == 0 and i // 2 + 4 < PAIRS:
+            if i % 2 == 0 and i // 2 + 4 < PAIRS and i >= 0:
                 load_x(i // 2 + 4)
-            if i < TILES:
-                widen(i)
-                turn(i)
-                empty(i)
+            for stage, lag in STAGES:
+                if 0 <= i - lag < TILES:
+                    stage(i - lag)
             if i == 1:
                 prepare_w()
-            if 0 <= i - 1 < TILES:
-                quant(i - 1)
-                mm1(i - 1)
-                empty_j(i - 1)
-            if 0 <= i - 2 < TILES:
-                quant_j(i - 2)
-                mm2(i - 2)
-            if 0 <= i - 3 < TILES:
-                add(i - 3)

@@ -47,7 +47,7 @@ def tile_mopn_layer_pb_t_w4_kernel(tc, hid_bytes, hid_scale, Wd, Wo_words, Wo_sc
         w_grp = keep.tile([P, 4, NS, 32, 4], BF16, align_bytes=64)
         w_codes = keep.tile([P, 4, NS, 32], U32, align_bytes=64)
         w_scales = keep.tile([P, 4 * P], U8, align_bytes=64)
-        wz_codes = keep.tile([P, 4, NS, P], U32, align_bytes=64)
+        wz_codes = keep.tile([P, 4, 640], U32, align_bytes=64)
         wo_words = keep.tile([P, 2 * D], U8, align_bytes=64)
         wo_scales = keep.tile([P, D], U8, align_bytes=64)
 
@@ -66,15 +66,14 @@ def tile_mopn_layer_pb_t_w4_kernel(tc, hid_bytes, hid_scale, Wd, Wo_words, Wo_sc
             nc.sync.dma_start(out=xt[:], in_=xin[j])
             xts[j] = xt
 
-        nc.sync.dma_start(out=scale[:, 0:H], in_=srow.partition_broadcast(P))
+        nc.sync.dma_start(out=scale_p[:], in_=srow.rearrange("(p t) -> p t", t=4))
         load_hid(0, 2)
         nc.sync.dma_start(out=w_raw[:].rearrange("p n j d -> p n (j d)"), in_=Wd.rearrange("n (p j) d -> p n (j d)", j=4))
         nc.gpsimd.memset(wo_scales[:].bitcast(I32), 0)
         make_identity(nc, ident[:])
         make_identity(nc, ident_b[:])
-        nc.gpsimd.memset(wz_codes[:].rearrange("p t n m -> p (t n m)").bitcast(I32), 0)
+        nc.gpsimd.memset(wz_codes[:].rearrange("p t z -> p (t z)").bitcast(I32), 0)
         load_hid(1)
-        nc.sync.dma_start(out=scale_p[:], in_=srow.rearrange("(p t) -> p t", t=4))
         nc.sync.dma_start(out=wo_words[:], in_=Wo_words[0])
         wos = Wo_scales[0].bitcast(I32)
         for q in range(4):
@@ -84,6 +83,10 @@ def tile_mopn_layer_pb_t_w4_kernel(tc, hid_bytes, hid_scale, Wd, Wo_words, Wo_sc
             load_hid(j)
             load_x(j - 1)
 
+        spread = pst.tile([P, 4, P], F32, name="po")
+        for t in range(4):
+            nc.tensor.transpose(spread[:, t, :], scale_p[:, t : t + 1].to_broadcast([P, P]), ident[:])
+        nc.vector.tensor_copy(out=scale[:, 0:H].rearrange("p (m t) -> p m t", t=4), in_=spread[:].rearrange("p t m -> p m t"))
         for n in range(1, NS):
             nc.scalar.copy(out=scale[:, n * H : (n + 1) * H], in_=scale[:, 0:H])
         for n in range(NS):
@@ -95,8 +98,9 @@ def tile_mopn_layer_pb_t_w4_kernel(tc, hid_bytes, hid_scale, Wd, Wo_words, Wo_sc
                 scales=w_scales[:],
                 in_=w_grp[:].rearrange("p t n m j -> p (t n m j)"),
             )
-            for n in range(NS):
-                nc.vector.tensor_copy(out=wz_codes[:, :, n, 32 * n : 32 * n + 32].bitcast(I32), in_=w_codes[:, :, n].bitcast(I32))
+            nc.vector.tensor_copy(
+                out=wz_codes[:].rearrange("p t (n z) -> p t n z", z=160)[:, :, :, 0:32].bitcast(I32), in_=w_codes[:].bitcast(I32)
+            )
 
         xs_t, xt_t, g_t, c_t, s_t, jp_t, jg_t, jc_t, js_t, po_t, o_t = ({} for z in range(11))
 
@@ -180,7 +184,7 @@ def tile_mopn_layer_pb_t_w4_kernel(tc, hid_bytes, hid_scale, Wd, Wo_words, Wo_sc
                 for n in range(NS):
                     nc.tensor.matmul_mx(
                         out=jp[:, t, :],
-                        lhsT=wz_codes[:, t, n, :].bitcast(F8X4),
+                        lhsT=wz_codes[:, t, P * n : P * (n + 1)].bitcast(F8X4),
                         lhsT_scale=w_scales[:, P * t : P * (t + 1)],
                         rhs=c_t[i][:, P * n : P * (n + 1)].bitcast(F8X4),
                         rhs_scale=s_t[i][:, P * n : P * (n + 1)],

import concourse.mybir as mybir
from concourse.masks import make_identity
from contextlib import ExitStack

F32 = mybir.dt.float32
BF16 = mybir.dt.bfloat16
U32 = mybir.dt.uint32
I32 = mybir.dt.int32
U8 = mybir.dt.uint8
F8 = mybir.dt.float8_e4m3fn
F8X4 = mybir.dt.float8_e4m3fn_x4
F4X4 = mybir.dt.float4_e2m1fn_x4
MULT = mybir.AluOpType.mult
ADD = mybir.AluOpType.add

P = 128
TOKENS = 4096
NS = 4
H = 512
DS = 128
D = NS * DS
TILES = TOKENS // P
PAIRS = TILES // 2
FLOPS = 2 * TOKENS * NS * H * DS + 2 * TOKENS * D * D


def tile_mopn_layer_pb_t_w4_kernel(tc, hid_bytes, hid_scale, Wd, Wo_words, Wo_scales, x, out):
    nc = tc.nc
    hid = hid_bytes.rearrange("b s n k -> (b s) (n k)").rearrange("(j p i) c -> j p (i c)", p=P, i=2)
    xin = x.rearrange("b s d -> (b s) d").rearrange("(j p i) c -> j p (i c)", p=P, i=2)
    oview = out.rearrange("b s d -> (b s) d").rearrange("(j p i) c -> j p (i c)", p=P, i=2)
    srow = hid_scale.rearrange("a b c k -> (a b c k)")

    with ExitStack() as ctx:
        keep = ctx.enter_context(tc.tile_pool(name="keep", bufs=1))
        loads = ctx.enter_context(tc.tile_pool(name="loads", bufs=8))
        sb = ctx.enter_context(tc.tile_pool(name="sb", bufs=4))
        pst = ctx.enter_context(tc.psum_pool(name="pst", bufs=2))

        ctx.enter_context(tc.manual_schedule())

        scale = keep.tile([P, NS * H], F32, align_bytes=64)
        scale_p = keep.tile([P, 4], F32, align_bytes=64)
        ident = keep.tile([P, P], F32, align_bytes=64)
        ident_b = keep.tile([P, P], BF16, align_bytes=64)
        w_raw = keep.tile([P, NS, 4, DS], BF16, align_bytes=64)
        w_grp = keep.tile([P, 4, NS, 32, 4], BF16, align_bytes=64)
        w_codes = keep.tile([P, 4, NS, 32], U32, align_bytes=64)
        w_scales = keep.tile([P, 4 * P], U8, align_bytes=64)
        wz_codes = keep.tile([P, 4, 640], U32, align_bytes=64)
        wo_words = keep.tile([P, 2 * D], U8, align_bytes=64)
        wo_scales = keep.tile([P, D], U8, align_bytes=64)

        hbs = {}
        xts = {}

        def load_hid(j, halves=1):
            hb = loads.tile([P, 4096], U8, align_bytes=64)
            w = 4096 // halves
            for h in range(halves):
                nc.sync.dma_start(out=hb[:, h * w : (h + 1) * w], in_=hid[j][:, h * w : (h + 1) * w])
            hbs[j] = hb

        def load_x(j):
            xt = loads.tile([P, 2 * D], BF16, align_bytes=64)
            nc.sync.dma_start(out=xt[:], in_=xin[j])
            xts[j] = xt

        nc.sync.dma_start(out=scale_p[:], in_=srow.rearrange("(p t) -> p t", t=4))
        load_hid(0, 2)
        nc.sync.dma_start(out=w_raw[:].rearrange("p n j d -> p n (j d)"), in_=Wd.rearrange("n (p j) d -> p n (j d)", j=4))
        nc.gpsimd.memset(wo_scales[:].bitcast(I32), 0)
        make_identity(nc, ident[:])
        make_identity(nc, ident_b[:])
        nc.gpsimd.memset(wz_codes[:].rearrange("p t z -> p (t z)").bitcast(I32), 0)
        load_hid(1)
        nc.sync.dma_start(out=wo_words[:], in_=Wo_words[0])
        wos = Wo_scales[0].bitcast(I32)
        for q in range(4):
            nc.sync.dma_start(out=wo_scales[32 * q : 32 * q + 4, :].bitcast(I32), in_=wos[4 * q : 4 * q + 4, :])
        load_x(0)
        for j in range(2, 5):
            load_hid(j)
            load_x(j - 1)

        spread = pst.tile([P, 4, P], F32, name="po")
        for t in range(4):
            nc.tensor.transpose(spread[:, t, :], scale_p[:, t : t + 1].to_broadcast([P, P]), ident[:])
        nc.vector.tensor_copy(out=scale[:, 0:H].rearrange("p (m t) -> p m t", t=4), in_=spread[:].rearrange("p t m -> p m t"))
        for n in range(1, NS):
            nc.scalar.copy(out=scale[:, n * H : (n + 1) * H], in_=scale[:, 0:H])
        for n in range(NS):
            nc.scalar.copy(out=w_grp[:, :, n], in_=w_raw[:, n].rearrange("p j (m t) -> p t m j", t=4))

        def prepare_w():
            nc.vector.quantize_mx(
                out=w_codes[:].rearrange("p t n m -> p (t n m)").bitcast(F8X4),
                scales=w_scales[:],
                in_=w_grp[:].rearrange("p t n m j -> p (t n m j)"),
            )
            nc.vector.tensor_copy(
                out=wz_codes[:].rearrange("p t (n z) -> p t n z", z=160)[:, :, :, 0:32].bitcast(I32), in_=w_codes[:].bitcast(I32)
            )

        xs_t, xt_t, g_t, c_t, s_t, jp_t, jg_t, jc_t, js_t, po_t, o_t = ({} for z in range(11))

        ws_t = {}

        def on_scalar(i):
            return 2 <= i < TILES - 2 and i % 3 != 1

        def widen_s(i):
            if not on_scalar(i):
                return
            ws = sb.tile([P, H], BF16, align_bytes=64)
            base = (i % 2) * NS * H + 3 * H
            nc.scalar.copy(out=ws[:], in_=hbs[i // 2][:, base : base + H].bitcast(F8))
            ws_t[i] = ws

        def widen(i):
            xs = sb.tile([P, NS * H], BF16, align_bytes=64)
            base = (i % 2) * NS * H
            hb = hbs[i // 2]
            w = 512 if i == 0 else 1024 if i == TILES - 1 else 1536 if on_scalar(i) else 2048
            for c in range(0, 3 * H if on_scalar(i) else 4 * H, w):
                nc.vector.tensor_tensor(
                    out=xs[:, c : c + w],
                    in0=hb[:, base + c : base + c + w].bitcast(F8),
                    in1=scale[:, 0:w],
                    op=MULT,
                )
            xs_t[i] = xs

        def turn(i):
            words = xs_t[i][:].bitcast(F32)
            banks = []
            for h in range(2):
                xt = pst.tile([P, 2, 2, P], F32, name="xt%d" % h)
                for a in range(2):
                    n = 2 * h + a
                    if n == 3 and on_scalar(i):
                        planes = xt[:, a].rearrange("p u r -> p (u r)").bitcast(BF16)
                        for t in range(4):
                            nc.tensor.transpose(planes[:, P * t : P * (t + 1)], ws_t[i][:, t::4], ident_b[:])
                        continue
                    for u in range(2):
                        nc.tensor.transpose(xt[:, a, u, :], words[:, 256 * n + u : 256 * (n + 1) : 2], ident[:])
                banks.append(xt)
            xt_t[i] = banks

        def empty(i):
            g = sb.tile([P, 2048], BF16, align_bytes=64)
            for h in range(2):
                if h == 1 and on_scalar(i):
                    nc.scalar.copy(
                        out=g[:, 1024:1536].bitcast(F32).rearrange("p (r u) -> p r u", u=2),
                        in_=xt_t[i][1][:, 0].rearrange("p u r -> p r u"),
                    )
                    planes = xt_t[i][1][:, 1].rearrange("p u r -> p (u r)").bitcast(BF16)
                    dst = g[:, 1536:2048].rearrange("p (r t) -> p r t", t=4)
                    for t in range(4):
                        nc.scalar.activation(
                            out=dst[:, :, t],
                            in_=planes[:, P * t : P * (t + 1)],
                            func=mybir.ActivationFunctionType.Copy,
                            scale=scale_p[:, t : t + 1],
                        )
                    continue
                nc.scalar.copy(
                    out=g[:, 1024 * h : 1024 * (h + 1)].bitcast(F32).rearrange("p (a r u) -> p a r u", a=2, u=2),
                    in_=xt_t[i][h][:].rearrange("p a u r -> p a r u"),
                )
            g_t[i] = g

        def quant(i):
            c = sb.tile([P, 512], U32, name="codes", align_bytes=64)
            s = sb.tile([P, 512], U8, name="scales", align_bytes=64)
            nc.vector.quantize_mx(out=c[:].bitcast(F8X4), scales=s[:], in_=g_t[i][:])
            c_t[i], s_t[i] = c, s

        def mm1(i):
            jp = pst.tile([P, 4, P], F32, name="jp")
            for t in range(4):
                for n in range(NS):
                    nc.tensor.matmul_mx(
                        out=jp[:, t, :],
                        lhsT=wz_codes[:, t, P * n : P * (n + 1)].bitcast(F8X4),
                        lhsT_scale=w_scales[:, P * t : P * (t + 1)],
                        rhs=c_t[i][:, P * n : P * (n + 1)].bitcast(F8X4),
                        rhs_scale=s_t[i][:, P * n : P * (n + 1)],
                        start=(n == 0),
                        stop=(n == NS - 1),
                    )
            jp_t[i] = jp

        def empty_j(i):
            jg = sb.tile([P, P, 4], BF16, name="jg", align_bytes=64)
            nc.scalar.copy(out=jg[:], in_=jp_t[i][:].rearrange("p t r -> p r t"))
            jg_t[i] = jg

        def quant_j(i):
            c = sb.tile([P, P], U32, name="jcodes", align_bytes=64)
            s = sb.tile([P, P], U8, name="jscales", align_bytes=64)
            nc.vector.quantize_mx(out=c[:].bitcast(F8X4), scales=s[:], in_=jg_t[i][:].rearrange("p r t -> p (r t)"))
            jc_t[i], js_t[i] = c, s

        def mm2(i):
            po = pst.tile([P, D], F32, name="po")
            nc.tensor.matmul_mx(
                out=po[:],
                lhsT=jc_t[i][:].bitcast(F8X4),
                lhsT_scale=js_t[i][:],
                rhs=wo_words[:].bitcast(F4X4),
                rhs_scale=wo_scales[:],
                start=True,
                stop=True,
            )
            po_t[i] = po

        def add(i):
            if i % 2 == 0:
                o_t[i // 2] = sb.tile([P, 2 * D], F32, name="o", align_bytes=64)
            o = o_t[i // 2]
            cols = slice((i % 2) * D, (i % 2 + 1) * D)
            nc.vector.tensor_tensor(out=o[:, cols], in0=po_t[i][:], in1=xts[i // 2][:, cols], op=ADD)
            if i >= TILES - 2:
                nc.sync.dma_start(out=oview[i // 2][:, cols], in_=o[:, cols])
            elif i % 2 == 1:
                nc.sync.dma_start(out=oview[i // 2], in_=o[:])

        STAGES = [(empty_j, 3), (widen_s, -1), (widen, 0), (add, 6), (quant, 2), (quant_j, 4), (turn, 0), (empty, 0), (mm1, 2), (mm2, 4)]
        for i in range(-1, TILES + 6):
            if i % 2 == 0 and i // 2 + 5 < PAIRS and i >= 0:
                load_hid(i // 2 + 5)
            if i % 2 == 0 and i // 2 + 4 < PAIRS and i >= 0:
                load_x(i // 2 + 4)
            for stage, lag in STAGES:
                if 0 <= i - lag < TILES:
                    stage(i - lag)
            if i == 1:
                prepare_w()
